import numpy as np
import ml_dtypes


def mxq(x, axis, fmt="e4m3"):
    dtype, down = {"e4m3": (ml_dtypes.float8_e4m3fn, 7), "e5m2": (ml_dtypes.float8_e5m2, 14)}[fmt]
    v = np.moveaxis(np.asarray(x, np.float32).astype(ml_dtypes.bfloat16).astype(np.float64), axis, -1)
    blocks = v.reshape(v.shape[:-1] + (-1, 32))
    amax = np.abs(blocks).max(-1, keepdims=True)
    byte = np.maximum(np.where(amax > 0, np.frexp(amax)[1] - 1 + 127, 0) - down, 1)
    scale = np.exp2(byte - 127.0)
    codes = (blocks / scale).astype(np.float32).astype(dtype).astype(np.float64)
    return np.moveaxis((codes * scale).reshape(v.shape), -1, axis)


WIDE = False


def mx_kscale(k):
    if not WIDE:
        return np.ones(k)
    levels = np.array([10, -10, 5, -5, 0])
    a = np.random.permutation(np.resize(levels, k // 512 * 4)).reshape(k // 512, 4)
    idx = np.arange(k)
    return np.exp2(a[idx // 512, idx % 128 // 32])


BF16 = ml_dtypes.bfloat16


def bf(x):
    return np.asarray(x, np.float32).astype(BF16)


def f64(x):
    return np.asarray(x).astype(np.float64)


E2M1 = np.array([0.0, 0.5, 1.0, 1.5, 2.0, 3.0, 4.0, 6.0, -0.0, -0.5, -1.0, -1.5, -2.0, -3.0, -4.0, -6.0])


def pack_weight(w, fmt):
    k, n = w.shape
    w = f64(bf(w)).reshape(k // 32, 32, n)
    amax = np.abs(w).max(1)
    if fmt == "e4m3":
        byte = np.frexp(amax)[1] - 1 + 127 - 7
    else:
        mant, ex = np.frexp(amax / 6.0)
        byte = np.where(mant > 0.5, ex, ex - 1) + 127
    byte = np.clip(np.where(amax > 0, byte, 1), 1, 254)
    scaled = (w * np.exp2(127.0 - byte)[:, None, :]).reshape(k, n).astype(np.float32)
    by_word = np.ascontiguousarray(scaled.reshape(k // 512, 128, 4, n).transpose(0, 1, 3, 2))
    if fmt == "e4m3":
        words = by_word.astype(ml_dtypes.float8_e4m3fn).view(np.uint8)
    else:
        c = by_word.astype(ml_dtypes.float4_e2m1fn).view(np.uint8) & 0xF
        words = c[..., 0::2] | (c[..., 1::2] << 4)
    return np.ascontiguousarray(words), np.ascontiguousarray(byte.astype(np.uint8).reshape(k // 512, 16, n))


def unpack_weight(words, scales, fmt):
    g, p, n, _ = words.shape
    if fmt == "e4m3":
        vals = np.ascontiguousarray(words).view(ml_dtypes.float8_e4m3fn).astype(np.float64)
    else:
        nib = np.empty((g, p, n, 4), np.uint8)
        nib[..., 0::2] = words & 0xF
        nib[..., 1::2] = words >> 4
        vals = E2M1[nib]
    vals = vals * np.repeat(np.exp2(scales.astype(np.float64) - 127.0), 8, axis=1)[..., None]
    return vals.transpose(0, 1, 3, 2).reshape(g * 512, n)

def pack4(w):
    words, scales = pack_weight(w, "e2m1")
    return words.reshape(words.shape[0], 128, -1), scales


def unpack4(words, scales):
    return unpack_weight(words.reshape(words.shape[0], 128, -1, 2), scales, "e2m1")


B, L, S, D, DA, H, MLP = 4, 3, 2048, 256, 512, 16, 4096
EPS = 1e-5


def layer_norm(u, g, b):
    mu = u.mean(-1, keepdims=True)
    var = ((u - mu) ** 2).mean(-1, keepdims=True)
    return (u - mu) / np.sqrt(var + EPS) * g + b


def setup_inputs():
    s = mx_kscale(DA)
    r = np.random.standard_normal
    h_attn = bf(r((B, S, DA)) * 2.0 * s)
    x = bf(r((B, S, D)))
    words, scales = pack4(r((DA, D)) * 0.5 / np.sqrt(DA) / s[:, None])
    return {"h_attn": h_attn, "x": x,
            "attn_out_W_words": words, "attn_out_W_scales": scales, "attn_out_b": bf(r(D) * 0.2),
            "attn_norm_g": bf(1.0 + 0.1 * r(D)), "attn_norm_b": bf(r(D) * 0.1)}


def reference(h_attn, x, attn_out_W_words, attn_out_W_scales, attn_out_b, attn_norm_g, attn_norm_b):
    o = (mxq(f64(h_attn), 2, "e4m3") @ unpack4(attn_out_W_words, attn_out_W_scales)) + f64(attn_out_b)
    return f64(x) + layer_norm(o, f64(attn_norm_g), f64(attn_norm_b))

@@ -1,0 +1,182 @@
+import concourse.mybir as mybir
+from concourse.masks import make_identity
+
+F32 = mybir.dt.float32
+BF16 = mybir.dt.bfloat16
+I32 = mybir.dt.int32
+U32 = mybir.dt.uint32
+U8 = mybir.dt.uint8
+FP8X4 = mybir.dt.float8_e4m3fn_x4
+FP4X4 = mybir.dt.float4_e2m1fn_x4
+ALU = mybir.AluOpType
+ACT = mybir.ActivationFunctionType
+
+P = 128
+TOKENS = 4 * 2048
+K = 512
+N = 256
+EPS = 1e-5
+GROUP = 4
+PAIR = 2
+GROUPS = TOKENS // (GROUP * P)
+WORDS = K // 2
+
+FLOPS = 2 * TOKENS * K * N
+
+
+def tile_dcadecoderblock_pb_t_kernel(
+    tc, h_attn, x, attn_out_W_words, attn_out_W_scales, attn_out_b, attn_norm_g, attn_norm_b, out
+):
+    nc = tc.nc
+
+    h_view = h_attn.flatten_outer_dims().rearrange("(g p j) k -> g p j k", p=P, j=GROUP)
+    x_view = x.flatten_outer_dims().rearrange("(g p j) n -> g p j n", p=P, j=GROUP)
+    out_view = out.flatten_outer_dims().rearrange("(g p j) n -> g p j n", p=P, j=GROUP)
+
+    with (
+        tc.tile_pool(name="const", bufs=1) as const,
+        tc.tile_pool(name="resident", bufs=GROUPS) as resident,
+        tc.tile_pool(name="work", bufs=3) as work,
+        tc.tile_pool(name="stats", bufs=4) as stats,
+        tc.psum_pool(name="psum_const", bufs=1) as psum_const,
+        tc.psum_pool(name="psum_xt", bufs=3) as psum_xt,
+        tc.psum_pool(name="psum_acc", bufs=3) as psum_acc,
+    ):
+        h_tiles = []
+        x_tiles = []
+        h_first = resident.tile([P, GROUP, K], BF16, name="h_sb")
+        nc.sync.dma_start(out=h_first[:], in_=h_view[0])
+        h_tiles.append(h_first)
+
+        w_words = const.tile([P, 2 * N], U8, align_bytes=64)
+        nc.sync.dma_start(
+            out=w_words[:].bitcast(I32),
+            in_=attn_out_W_words.rearrange("g p b -> (g p) b").bitcast(I32),
+        )
+        w_scales = const.tile([P, N], U8, align_bytes=64)
+        nc.vector.memset(w_scales[:].bitcast(I32), 0)
+        scale_rows = attn_out_W_scales.rearrange("g q n -> (g q) n")
+        for quadrant in range(4):
+            nc.sync.dma_start(
+                out=w_scales[32 * quadrant : 32 * quadrant + 4, :].bitcast(I32),
+                in_=scale_rows[4 * quadrant : 4 * quadrant + 4, :].bitcast(I32),
+            )
+
+        rows = const.tile([P, 3 * N], BF16)
+        nc.vector.memset(rows[:], 0.0)
+        nc.scalar.dma_start(out=rows[0:1, 0:N], in_=attn_out_b.unsqueeze(0))
+        nc.scalar.dma_start(out=rows[0:1, N : 2 * N], in_=attn_norm_b.unsqueeze(0))
+        nc.scalar.dma_start(out=rows[0:1, 2 * N : 3 * N], in_=attn_norm_g.unsqueeze(0))
+
+        for g in range(GROUPS):
+            if g > 0:
+                h_sb = resident.tile([P, GROUP, K], BF16, name="h_sb")
+                nc.sync.dma_start(out=h_sb[:], in_=h_view[g])
+                h_tiles.append(h_sb)
+            x_sb = resident.tile([P, GROUP, N], BF16, name="x_sb")
+            nc.sync.dma_start(out=x_sb[:], in_=x_view[g])
+            x_tiles.append(x_sb)
+
+        ident = const.tile([P, P], F32)
+        make_identity(nc, ident[:])
+        ones = const.tile([P, P], BF16)
+        nc.vector.memset(ones[:], 1.0)
+        eps = const.tile([P, 1], F32)
+        nc.vector.memset(eps[:], EPS)
+        warm = const.tile([P, 1], F32)
+        nc.scalar.activation(out=warm[:], in_=eps[:], func=ACT.Sqrt)
+
+        spread = psum_acc.tile([P, PAIR, N], F32, name="acc")
+        nc.tensor.matmul(
+            out=spread[:].rearrange("p a n -> p (a n)"), lhsT=ones[:], rhs=rows[:, 0 : 2 * N],
+            start=True, stop=True,
+        )
+        bias_shift = const.tile([P, PAIR, N], F32)
+        nc.vector.tensor_copy(out=bias_shift[:], in_=spread[:])
+        bias_bc = bias_shift[:, 0:1, :]
+        shift_bc = bias_shift[:, 1:2, :]
+        gain_bc = psum_const.tile([P, N], F32)
+        nc.tensor.matmul(out=gain_bc[:], lhsT=ones[:], rhs=rows[:, 2 * N : 3 * N], start=True, stop=True)
+
+        for g in range(GROUPS):
+            h_words = h_tiles[g][:].bitcast(F32)
+
+            o_sb = resident.tile([P, GROUP, N], F32, name="o_sb")
+            nc.gpsimd.tensor_tensor(
+                out=o_sb[:], in0=x_tiles[g][:], in1=shift_bc.to_broadcast([P, GROUP, N]), op=ALU.add
+            )
+
+            grouped = work.tile([P, GROUP * P * 4], BF16, align_bytes=64)
+            grouped_words = grouped[:].bitcast(F32)
+            for pair in range(GROUP // PAIR):
+                xt = psum_xt.tile([P, 2, PAIR * P], F32)
+                for jj in range(PAIR):
+                    for u in range(2):
+                        nc.tensor.transpose(
+                            xt[:, u, jj * P : (jj + 1) * P],
+                            h_words[:, pair * PAIR + jj, u:WORDS:2],
+                            ident[:],
+                        )
+                nc.scalar.copy(
+                    out=grouped_words[:, pair * 4 * P : (pair + 1) * 4 * P].rearrange(
+                        "p (c u) -> p c u", u=2
+                    ),
+                    in_=xt[:].rearrange("p u c -> p c u"),
+                )
+
+            codes = work.tile([P, GROUP * P], U32, align_bytes=64)
+            scales = work.tile([P, GROUP * P], U8, align_bytes=64)
+            nc.vector.quantize_mx(out=codes[:].bitcast(FP8X4), scales=scales[:], in_=grouped[:])
+
+            t = work.tile([P, GROUP, N], F32)
+            for pair in range(GROUP // PAIR):
+                acc = psum_acc.tile([P, PAIR, N], F32)
+                for jj in range(PAIR):
+                    cols = slice((pair * PAIR + jj) * P, (pair * PAIR + jj + 1) * P)
+                    nc.tensor.matmul_mx(
+                        out=acc[:, jj, :],
+                        lhsT=codes[:, cols].bitcast(FP8X4),
+                        lhsT_scale=scales[:, cols],
+                        rhs=w_words[:].bitcast(FP4X4),
+                        rhs_scale=w_scales[:],
+                        start=True,
+                        stop=True,
+                    )
+                nc.vector.tensor_tensor(
+                    out=t[:, pair * PAIR : (pair + 1) * PAIR, :],
+                    in0=acc[:],
+                    in1=bias_bc.to_broadcast([P, PAIR, N]),
+                    op=ALU.add,
+                )
+
+            neg_mean = stats.tile([P, GROUP], F32)
+            sum_sq = stats.tile([P, GROUP], F32)
+            for j in range(GROUP):
+                unread = stats.tile([P, N], BF16, name="unread")
+                nc.scalar.activation(
+                    out=unread[:], in_=t[:, j, :], func=ACT.Identity, scale=-1.0 / N,
+                    accum_out=neg_mean[:, j : j + 1],
+                )
+            for j in range(GROUP):
+                unread = stats.tile([P, N], BF16, name="unread")
+                nc.scalar.activation(
+                    out=unread[:], in_=t[:, j, :], func=ACT.Square, bias=neg_mean[:, j : j + 1],
+                    accum_out=sum_sq[:, j : j + 1],
+                )
+            std = stats.tile([P, GROUP], F32)
+            nc.scalar.activation(out=std[:], in_=sum_sq[:], func=ACT.Sqrt, scale=1.0 / N, bias=eps[:])
+            rstd = stats.tile([P, GROUP], F32)
+            nc.vector.reciprocal(out=rstd[:], in_=std[:])
+
+            centred = work.tile([P, GROUP, N], F32)
+            for j in range(GROUP):
+                nc.vector.scalar_tensor_tensor(
+                    out=centred[:, j, :], in0=t[:, j, :], scalar=neg_mean[:, j : j + 1], in1=gain_bc[:],
+                    op0=ALU.add, op1=ALU.mult,
+                )
+            for j in range(GROUP):
+                nc.vector.scalar_tensor_tensor(
+                    out=o_sb[:, j, :], in0=centred[:, j, :], scalar=rstd[:, j : j + 1], in1=o_sb[:, j, :],
+                    op0=ALU.mult, op1=ALU.add,
+                )
+            nc.sync.dma_start(out=out_view[g], in_=o_sb[:])

@@ -87,24 +87,19 @@ def tile_dcadecoderblock_pb_t_kernel(
         nc.scalar.activation(out=warm[:], in_=eps[:], func=ACT.Sqrt)
 
         spread = psum_acc.tile([P, PAIR, N], F32, name="acc")
+        nc.tensor.matmul(out=spread[:, 0, :], lhsT=ones[:], rhs=rows[:, 0:N], start=True, stop=True)
+        bias_bc = const.tile([P, 1, N], F32)
+        nc.vector.tensor_copy(out=bias_bc[:, 0, :], in_=spread[:, 0, :])
+        shift_gain = psum_const.tile([P, 2, N], F32)
         nc.tensor.matmul(
-            out=spread[:].rearrange("p a n -> p (a n)"), lhsT=ones[:], rhs=rows[:, 0 : 2 * N],
+            out=shift_gain[:].rearrange("p a n -> p (a n)"), lhsT=ones[:], rhs=rows[:, N : 3 * N],
             start=True, stop=True,
         )
-        bias_shift = const.tile([P, PAIR, N], F32)
-        nc.vector.tensor_copy(out=bias_shift[:], in_=spread[:])
-        bias_bc = bias_shift[:, 0:1, :]
-        shift_bc = bias_shift[:, 1:2, :]
-        gain_bc = psum_const.tile([P, N], F32)
-        nc.tensor.matmul(out=gain_bc[:], lhsT=ones[:], rhs=rows[:, 2 * N : 3 * N], start=True, stop=True)
+        shift_bc = shift_gain[:, 0, :]
+        gain_bc = shift_gain[:, 1, :]
 
         for g in range(GROUPS):
             h_words = h_tiles[g][:].bitcast(F32)
-
-            o_sb = resident.tile([P, GROUP, N], F32, name="o_sb")
-            nc.gpsimd.tensor_tensor(
-                out=o_sb[:], in0=x_tiles[g][:], in1=shift_bc.to_broadcast([P, GROUP, N]), op=ALU.add
-            )
 
             grouped = work.tile([P, GROUP * P * 4], BF16, align_bytes=64)
             grouped_words = grouped[:].bitcast(F32)
@@ -145,7 +140,7 @@ def tile_dcadecoderblock_pb_t_kernel(
                 nc.vector.tensor_tensor(
                     out=t[:, pair * PAIR : (pair + 1) * PAIR, :],
                     in0=acc[:],
-                    in1=bias_bc.to_broadcast([P, PAIR, N]),
+                    in1=bias_bc[:].to_broadcast([P, PAIR, N]),
                     op=ALU.add,
                 )
 
@@ -171,12 +166,16 @@ def tile_dcadecoderblock_pb_t_kernel(
             centred = work.tile([P, GROUP, N], F32)
             for j in range(GROUP):
                 nc.vector.scalar_tensor_tensor(
-                    out=centred[:, j, :], in0=t[:, j, :], scalar=neg_mean[:, j : j + 1], in1=gain_bc[:],
+                    out=centred[:, j, :], in0=t[:, j, :], scalar=neg_mean[:, j : j + 1], in1=gain_bc,
                     op0=ALU.add, op1=ALU.mult,
                 )
+            o_sb = work.tile([P, GROUP, N], F32)
             for j in range(GROUP):
                 nc.vector.scalar_tensor_tensor(
-                    out=o_sb[:, j, :], in0=centred[:, j, :], scalar=rstd[:, j : j + 1], in1=o_sb[:, j, :],
+                    out=o_sb[:, j, :], in0=centred[:, j, :], scalar=rstd[:, j : j + 1], in1=shift_bc,
                     op0=ALU.mult, op1=ALU.add,
+                )
+                nc.gpsimd.tensor_tensor(
+                    out=o_sb[:, j, :], in0=o_sb[:, j, :], in1=x_tiles[g][:, j, :], op=ALU.add
                 )
             nc.sync.dma_start(out=out_view[g], in_=o_sb[:])

@@ -19,6 +19,7 @@ EPS = 1e-5
 GROUP = 4
 PAIR = 2
 GROUPS = TOKENS // (GROUP * P)
+X_LAG = 4
 WORDS = K // 2
 
 FLOPS = 2 * TOKENS * K * N
@@ -36,18 +37,25 @@ def tile_dcadecoderblock_pb_t_kernel(
     with (
         tc.tile_pool(name="const", bufs=1) as const,
         tc.tile_pool(name="resident", bufs=GROUPS) as resident,
-        tc.tile_pool(name="work", bufs=3) as work,
+        tc.tile_pool(name="work", bufs=4) as work,
         tc.tile_pool(name="stats", bufs=4) as stats,
         tc.psum_pool(name="psum_const", bufs=1) as psum_const,
         tc.psum_pool(name="psum_xt", bufs=3) as psum_xt,
-        tc.psum_pool(name="psum_acc", bufs=3) as psum_acc,
+        tc.psum_pool(name="psum_acc", bufs=4) as psum_acc,
+        tc.manual_schedule(),
     ):
-        h_tiles = []
-        x_tiles = []
-        h_first = resident.tile([P, GROUP, K], BF16, name="h_sb")
-        nc.sync.dma_start(out=h_first[:], in_=h_view[0])
-        h_tiles.append(h_first)
+        h_of, x_of, banks_of, grouped_of, codes_of, scales_of = {}, {}, {}, {}, {}, {}
+        acc_of, t_of, neg_mean_of, std_of, rstd_of, centred_of = {}, {}, {}, {}, {}, {}
 
+        def load_h(g):
+            h_of[g] = resident.tile([P, GROUP, K], BF16, name="h_sb")
+            nc.sync.dma_start(out=h_of[g][:], in_=h_view[g])
+
+        def load_x(g):
+            x_of[g] = resident.tile([P, GROUP, N], BF16, name="x_sb")
+            nc.sync.dma_start(out=x_of[g][:], in_=x_view[g])
+
+        load_h(0)
         w_words = const.tile([P, 2 * N], U8, align_bytes=64)
         nc.sync.dma_start(
             out=w_words[:].bitcast(I32),
@@ -61,22 +69,17 @@ def tile_dcadecoderblock_pb_t_kernel(
                 out=w_scales[32 * quadrant : 32 * quadrant + 4, :].bitcast(I32),
                 in_=scale_rows[4 * quadrant : 4 * quadrant + 4, :].bitcast(I32),
             )
+        for g in range(1, GROUPS + X_LAG):
+            if g < GROUPS:
+                load_h(g)
+            if g >= X_LAG:
+                load_x(g - X_LAG)
 
         rows = const.tile([P, 3 * N], BF16)
         nc.vector.memset(rows[:], 0.0)
         nc.scalar.dma_start(out=rows[0:1, 0:N], in_=attn_out_b.unsqueeze(0))
         nc.scalar.dma_start(out=rows[0:1, N : 2 * N], in_=attn_norm_b.unsqueeze(0))
         nc.scalar.dma_start(out=rows[0:1, 2 * N : 3 * N], in_=attn_norm_g.unsqueeze(0))
-
-        for g in range(GROUPS):
-            if g > 0:
-                h_sb = resident.tile([P, GROUP, K], BF16, name="h_sb")
-                nc.sync.dma_start(out=h_sb[:], in_=h_view[g])
-                h_tiles.append(h_sb)
-            x_sb = resident.tile([P, GROUP, N], BF16, name="x_sb")
-            nc.sync.dma_start(out=x_sb[:], in_=x_view[g])
-            x_tiles.append(x_sb)
-
         ident = const.tile([P, P], F32)
         make_identity(nc, ident[:])
         ones = const.tile([P, P], BF16)
@@ -98,13 +101,12 @@ def tile_dcadecoderblock_pb_t_kernel(
         shift_bc = shift_gain[:, 0, :]
         gain_bc = shift_gain[:, 1, :]
 
-        for g in range(GROUPS):
-            h_words = h_tiles[g][:].bitcast(F32)
-
-            grouped = work.tile([P, GROUP * P * 4], BF16, align_bytes=64)
-            grouped_words = grouped[:].bitcast(F32)
+        def transpose(g):
+            h_words = h_of[g][:].bitcast(F32)
+            banks_of[g] = []
             for pair in range(GROUP // PAIR):
                 xt = psum_xt.tile([P, 2, PAIR * P], F32)
+                banks_of[g].append(xt)
                 for jj in range(PAIR):
                     for u in range(2):
                         nc.tensor.transpose(
@@ -112,70 +114,116 @@ def tile_dcadecoderblock_pb_t_kernel(
                             h_words[:, pair * PAIR + jj, u:WORDS:2],
                             ident[:],
                         )
+
+        def regroup(g):
+            grouped_of[g] = work.tile([P, GROUP * P * 4], BF16, align_bytes=64, name="grouped")
+            grouped_words = grouped_of[g][:].bitcast(F32)
+            for pair in range(GROUP // PAIR):
                 nc.scalar.copy(
                     out=grouped_words[:, pair * 4 * P : (pair + 1) * 4 * P].rearrange(
                         "p (c u) -> p c u", u=2
                     ),
-                    in_=xt[:].rearrange("p u c -> p c u"),
+                    in_=banks_of[g][pair][:].rearrange("p u c -> p c u"),
                 )
 
-            codes = work.tile([P, GROUP * P], U32, align_bytes=64)
-            scales = work.tile([P, GROUP * P], U8, align_bytes=64)
-            nc.vector.quantize_mx(out=codes[:].bitcast(FP8X4), scales=scales[:], in_=grouped[:])
+        def quantise(g):
+            codes_of[g] = work.tile([P, GROUP * P], U32, align_bytes=64, name="codes")
+            scales_of[g] = work.tile([P, GROUP * P], U8, align_bytes=64, name="scales")
+            nc.vector.quantize_mx(
+                out=codes_of[g][:].bitcast(FP8X4), scales=scales_of[g][:], in_=grouped_of[g][:]
+            )
 
-            t = work.tile([P, GROUP, N], F32)
+        def project(g):
+            acc_of[g] = []
             for pair in range(GROUP // PAIR):
                 acc = psum_acc.tile([P, PAIR, N], F32)
+                acc_of[g].append(acc)
                 for jj in range(PAIR):
                     cols = slice((pair * PAIR + jj) * P, (pair * PAIR + jj + 1) * P)
                     nc.tensor.matmul_mx(
                         out=acc[:, jj, :],
-                        lhsT=codes[:, cols].bitcast(FP8X4),
-                        lhsT_scale=scales[:, cols],
+                        lhsT=codes_of[g][:, cols].bitcast(FP8X4),
+                        lhsT_scale=scales_of[g][:, cols],
                         rhs=w_words[:].bitcast(FP4X4),
                         rhs_scale=w_scales[:],
                         start=True,
                         stop=True,
                     )
+
+        def add_bias(g):
+            t_of[g] = work.tile([P, GROUP, N], F32, name="t")
+            for pair in range(GROUP // PAIR):
                 nc.vector.tensor_tensor(
-                    out=t[:, pair * PAIR : (pair + 1) * PAIR, :],
-                    in0=acc[:],
+                    out=t_of[g][:, pair * PAIR : (pair + 1) * PAIR, :],
+                    in0=acc_of[g][pair][:],
                     in1=bias_bc[:].to_broadcast([P, PAIR, N]),
                     op=ALU.add,
                 )
 
-            neg_mean = stats.tile([P, GROUP], F32)
+        def mean(g):
+            neg_mean_of[g] = stats.tile([P, GROUP], F32, name="neg_mean")
+            for j in range(GROUP):
+                unread = stats.tile([P, N], BF16, name="unread")
+                nc.scalar.activation(
+                    out=unread[:], in_=t_of[g][:, j, :], func=ACT.Identity, scale=-1.0 / N,
+                    accum_out=neg_mean_of[g][:, j : j + 1],
+                )
+
+        def centre_and_gain(g):
+            centred_of[g] = work.tile([P, GROUP, N], F32, name="centred")
+            for j in range(GROUP):
+                nc.vector.scalar_tensor_tensor(
+                    out=centred_of[g][:, j, :], in0=t_of[g][:, j, :],
+                    scalar=neg_mean_of[g][:, j : j + 1], in1=gain_bc,
+                    op0=ALU.add, op1=ALU.mult,
+                )
+
+        def deviation(g):
             sum_sq = stats.tile([P, GROUP], F32)
             for j in range(GROUP):
                 unread = stats.tile([P, N], BF16, name="unread")
                 nc.scalar.activation(
-                    out=unread[:], in_=t[:, j, :], func=ACT.Identity, scale=-1.0 / N,
-                    accum_out=neg_mean[:, j : j + 1],
+                    out=unread[:], in_=t_of[g][:, j, :], func=ACT.Square,
+                    bias=neg_mean_of[g][:, j : j + 1], accum_out=sum_sq[:, j : j + 1],
                 )
-            for j in range(GROUP):
-                unread = stats.tile([P, N], BF16, name="unread")
-                nc.scalar.activation(
-                    out=unread[:], in_=t[:, j, :], func=ACT.Square, bias=neg_mean[:, j : j + 1],
-                    accum_out=sum_sq[:, j : j + 1],
-                )
-            std = stats.tile([P, GROUP], F32)
-            nc.scalar.activation(out=std[:], in_=sum_sq[:], func=ACT.Sqrt, scale=1.0 / N, bias=eps[:])
-            rstd = stats.tile([P, GROUP], F32)
-            nc.vector.reciprocal(out=rstd[:], in_=std[:])
+            std_of[g] = stats.tile([P, GROUP], F32, name="std")
+            nc.scalar.activation(
+                out=std_of[g][:], in_=sum_sq[:], func=ACT.Sqrt, scale=1.0 / N, bias=eps[:]
+            )
 
-            centred = work.tile([P, GROUP, N], F32)
-            for j in range(GROUP):
-                nc.vector.scalar_tensor_tensor(
-                    out=centred[:, j, :], in0=t[:, j, :], scalar=neg_mean[:, j : j + 1], in1=gain_bc,
-                    op0=ALU.add, op1=ALU.mult,
-                )
+        def invert(g):
+            rstd_of[g] = stats.tile([P, GROUP], F32, name="rstd")
+            nc.vector.reciprocal(out=rstd_of[g][:], in_=std_of[g][:])
+
+        def finish(g):
             o_sb = work.tile([P, GROUP, N], F32)
             for j in range(GROUP):
                 nc.vector.scalar_tensor_tensor(
-                    out=o_sb[:, j, :], in0=centred[:, j, :], scalar=rstd[:, j : j + 1], in1=shift_bc,
-                    op0=ALU.mult, op1=ALU.add,
+                    out=o_sb[:, j, :], in0=centred_of[g][:, j, :], scalar=rstd_of[g][:, j : j + 1],
+                    in1=shift_bc, op0=ALU.mult, op1=ALU.add,
                 )
                 nc.gpsimd.tensor_tensor(
-                    out=o_sb[:, j, :], in0=o_sb[:, j, :], in1=x_tiles[g][:, j, :], op=ALU.add
+                    out=o_sb[:, j, :], in0=o_sb[:, j, :], in1=x_of[g][:, j, :], op=ALU.add
                 )
             nc.sync.dma_start(out=out_view[g], in_=o_sb[:])
+
+        def live(g):
+            return 0 <= g < GROUPS
+
+        for r in range(GROUPS + 5):
+            if live(r - 1):
+                regroup(r - 1)
+            if live(r):
+                transpose(r)
+            if live(r - 2):
+                quantise(r - 2)
+                project(r - 2)
+            if live(r - 3):
+                add_bias(r - 3)
+            if live(r - 4):
+                mean(r - 4)
+                deviation(r - 4)
+            if live(r - 5):
+                invert(r - 5)
+                centre_and_gain(r - 5)
+                finish(r - 5)

@@ -44,7 +44,7 @@ def tile_dcadecoderblock_pb_t_kernel(
         tc.psum_pool(name="psum_acc", bufs=4) as psum_acc,
         tc.manual_schedule(),
     ):
-        h_of, x_of, banks_of, grouped_of, codes_of, scales_of = {}, {}, {}, {}, {}, {}
+        h_of, x_of, o_of, banks_of, grouped_of, codes_of, scales_of = {}, {}, {}, {}, {}, {}, {}
         acc_of, t_of, neg_mean_of, std_of, rstd_of, centred_of = {}, {}, {}, {}, {}, {}
 
         def load_h(g):
@@ -90,16 +90,24 @@ def tile_dcadecoderblock_pb_t_kernel(
         nc.scalar.activation(out=warm[:], in_=eps[:], func=ACT.Sqrt)
 
         spread = psum_acc.tile([P, PAIR, N], F32, name="acc")
-        nc.tensor.matmul(out=spread[:, 0, :], lhsT=ones[:], rhs=rows[:, 0:N], start=True, stop=True)
-        bias_bc = const.tile([P, 1, N], F32)
-        nc.vector.tensor_copy(out=bias_bc[:, 0, :], in_=spread[:, 0, :])
-        shift_gain = psum_const.tile([P, 2, N], F32)
         nc.tensor.matmul(
-            out=shift_gain[:].rearrange("p a n -> p (a n)"), lhsT=ones[:], rhs=rows[:, N : 3 * N],
+            out=spread[:].rearrange("p a n -> p (a n)"), lhsT=ones[:], rhs=rows[:, 0 : 2 * N],
             start=True, stop=True,
         )
-        shift_bc = shift_gain[:, 0, :]
-        gain_bc = shift_gain[:, 1, :]
+        bias_shift = const.tile([P, PAIR, N], F32)
+        nc.vector.tensor_copy(out=bias_shift[:], in_=spread[:])
+        bias_bc = bias_shift[:, 0:1, :]
+        shift_bc = bias_shift[:, 1, :]
+        gain_ps = psum_const.tile([P, N], F32)
+        nc.tensor.matmul(out=gain_ps[:], lhsT=ones[:], rhs=rows[:, 2 * N : 3 * N], start=True, stop=True)
+        gain_bc = gain_ps[:]
+
+        def add_shift(g):
+            o_of[g] = resident.tile([P, GROUP, N], F32, name="o_sb")
+            for j in range(GROUP):
+                nc.gpsimd.tensor_tensor(
+                    out=o_of[g][:, j, :], in0=x_of[g][:, j, :], in1=shift_bc, op=ALU.add
+                )
 
         def transpose(g):
             h_words = h_of[g][:].bitcast(F32)
@@ -156,7 +164,7 @@ def tile_dcadecoderblock_pb_t_kernel(
                 nc.vector.tensor_tensor(
                     out=t_of[g][:, pair * PAIR : (pair + 1) * PAIR, :],
                     in0=acc_of[g][pair][:],
-                    in1=bias_bc[:].to_broadcast([P, PAIR, N]),
+                    in1=bias_bc.to_broadcast([P, PAIR, N]),
                     op=ALU.add,
                 )
 
@@ -196,16 +204,12 @@ def tile_dcadecoderblock_pb_t_kernel(
             nc.vector.reciprocal(out=rstd_of[g][:], in_=std_of[g][:])
 
         def finish(g):
-            o_sb = work.tile([P, GROUP, N], F32)
             for j in range(GROUP):
                 nc.vector.scalar_tensor_tensor(
-                    out=o_sb[:, j, :], in0=centred_of[g][:, j, :], scalar=rstd_of[g][:, j : j + 1],
-                    in1=shift_bc, op0=ALU.mult, op1=ALU.add,
+                    out=o_of[g][:, j, :], in0=centred_of[g][:, j, :], scalar=rstd_of[g][:, j : j + 1],
+                    in1=o_of[g][:, j, :], op0=ALU.mult, op1=ALU.add,
                 )
-                nc.gpsimd.tensor_tensor(
-                    out=o_sb[:, j, :], in0=o_sb[:, j, :], in1=x_of[g][:, j, :], op=ALU.add
-                )
-            nc.sync.dma_start(out=out_view[g], in_=o_sb[:])
+            nc.sync.dma_start(out=out_view[g], in_=o_of[g][:])
 
         def live(g):
             return 0 <= g < GROUPS
@@ -215,6 +219,7 @@ def tile_dcadecoderblock_pb_t_kernel(
                 regroup(r - 1)
             if live(r):
                 transpose(r)
+                add_shift(r)
             if live(r - 2):
                 quantise(r - 2)
                 project(r - 2)

@@ -44,8 +44,8 @@ def tile_dcadecoderblock_pb_t_kernel(
         tc.psum_pool(name="psum_acc", bufs=4) as psum_acc,
         tc.manual_schedule(),
     ):
-        h_of, x_of, o_of, banks_of, grouped_of, codes_of, scales_of = {}, {}, {}, {}, {}, {}, {}
-        acc_of, t_of, neg_mean_of, std_of, rstd_of, centred_of = {}, {}, {}, {}, {}, {}
+        h_of, x_of, banks_of, grouped_of, codes_of, scales_of = {}, {}, {}, {}, {}, {}
+        acc_of, t_of, neg_mean_of, rstd_of, centred_of = {}, {}, {}, {}, {}
 
         def load_h(g):
             h_of[g] = resident.tile([P, GROUP, K], BF16, name="h_sb")
@@ -87,27 +87,19 @@ def tile_dcadecoderblock_pb_t_kernel(
         eps = const.tile([P, 1], F32)
         nc.vector.memset(eps[:], EPS)
         warm = const.tile([P, 1], F32)
-        nc.scalar.activation(out=warm[:], in_=eps[:], func=ACT.Sqrt)
+        nc.scalar.activation(out=warm[:], in_=eps[:], func=ACT.Abs_reciprocal_sqrt)
 
         spread = psum_acc.tile([P, PAIR, N], F32, name="acc")
+        nc.tensor.matmul(out=spread[:, 0, :], lhsT=ones[:], rhs=rows[:, 0:N], start=True, stop=True)
+        bias_bc = const.tile([P, 1, N], F32)
+        nc.vector.tensor_copy(out=bias_bc[:, 0, :], in_=spread[:, 0, :])
+        shift_gain = psum_const.tile([P, 2, N], F32)
         nc.tensor.matmul(
-            out=spread[:].rearrange("p a n -> p (a n)"), lhsT=ones[:], rhs=rows[:, 0 : 2 * N],
+            out=shift_gain[:].rearrange("p a n -> p (a n)"), lhsT=ones[:], rhs=rows[:, N : 3 * N],
             start=True, stop=True,
         )
-        bias_shift = const.tile([P, PAIR, N], F32)
-        nc.vector.tensor_copy(out=bias_shift[:], in_=spread[:])
-        bias_bc = bias_shift[:, 0:1, :]
-        shift_bc = bias_shift[:, 1, :]
-        gain_ps = psum_const.tile([P, N], F32)
-        nc.tensor.matmul(out=gain_ps[:], lhsT=ones[:], rhs=rows[:, 2 * N : 3 * N], start=True, stop=True)
-        gain_bc = gain_ps[:]
-
-        def add_shift(g):
-            o_of[g] = resident.tile([P, GROUP, N], F32, name="o_sb")
-            for j in range(GROUP):
-                nc.gpsimd.tensor_tensor(
-                    out=o_of[g][:, j, :], in0=x_of[g][:, j, :], in1=shift_bc, op=ALU.add
-                )
+        shift_bc = shift_gain[:, 0, :]
+        gain_bc = shift_gain[:, 1, :]
 
         def transpose(g):
             h_words = h_of[g][:].bitcast(F32)
@@ -164,7 +156,7 @@ def tile_dcadecoderblock_pb_t_kernel(
                 nc.vector.tensor_tensor(
                     out=t_of[g][:, pair * PAIR : (pair + 1) * PAIR, :],
                     in0=acc_of[g][pair][:],
-                    in1=bias_bc.to_broadcast([P, PAIR, N]),
+                    in1=bias_bc[:].to_broadcast([P, PAIR, N]),
                     op=ALU.add,
                 )
 
@@ -194,41 +186,42 @@ def tile_dcadecoderblock_pb_t_kernel(
                     out=unread[:], in_=t_of[g][:, j, :], func=ACT.Square,
                     bias=neg_mean_of[g][:, j : j + 1], accum_out=sum_sq[:, j : j + 1],
                 )
-            std_of[g] = stats.tile([P, GROUP], F32, name="std")
+            rstd_of[g] = stats.tile([P, GROUP], F32, name="rstd")
             nc.scalar.activation(
-                out=std_of[g][:], in_=sum_sq[:], func=ACT.Sqrt, scale=1.0 / N, bias=eps[:]
+                out=rstd_of[g][:], in_=sum_sq[:], func=ACT.Abs_reciprocal_sqrt, scale=1.0 / N, bias=eps[:]
             )
 
-        def invert(g):
-            rstd_of[g] = stats.tile([P, GROUP], F32, name="rstd")
-            nc.vector.reciprocal(out=rstd_of[g][:], in_=std_of[g][:])
-
         def finish(g):
-            for j in range(GROUP):
-                nc.vector.scalar_tensor_tensor(
-                    out=o_of[g][:, j, :], in0=centred_of[g][:, j, :], scalar=rstd_of[g][:, j : j + 1],
-                    in1=o_of[g][:, j, :], op0=ALU.mult, op1=ALU.add,
+            o_sb = work.tile([P, GROUP, N], F32)
+            for pair in range(GROUP // PAIR):
+                tiles = slice(pair * PAIR, (pair + 1) * PAIR)
+                for j in range(pair * PAIR, (pair + 1) * PAIR):
+                    nc.vector.scalar_tensor_tensor(
+                        out=o_sb[:, j, :], in0=centred_of[g][:, j, :], scalar=rstd_of[g][:, j : j + 1],
+                        in1=shift_bc, op0=ALU.mult, op1=ALU.add,
+                    )
+                nc.gpsimd.tensor_tensor(
+                    out=o_sb[:, tiles, :], in0=o_sb[:, tiles, :], in1=x_of[g][:, tiles, :], op=ALU.add
                 )
-            nc.sync.dma_start(out=out_view[g], in_=o_of[g][:])
+                nc.sync.dma_start(out=out_view[g][:, tiles, :], in_=o_sb[:, tiles, :])
 
         def live(g):
             return 0 <= g < GROUPS
 
         for r in range(GROUPS + 5):
+            if live(r - 5):
+                deviation(r - 5)
             if live(r - 1):
                 regroup(r - 1)
             if live(r):
                 transpose(r)
-                add_shift(r)
+            if live(r - 4):
+                add_bias(r - 4)
+                mean(r - 4)
+            if live(r - 5):
+                centre_and_gain(r - 5)
             if live(r - 2):
                 quantise(r - 2)
                 project(r - 2)
-            if live(r - 3):
-                add_bias(r - 3)
-            if live(r - 4):
-                mean(r - 4)
-                deviation(r - 4)
             if live(r - 5):
-                invert(r - 5)
-                centre_and_gain(r - 5)
                 finish(r - 5)

@@ -20,6 +20,7 @@ GROUP = 4
 PAIR = 2
 GROUPS = TOKENS // (GROUP * P)
 X_LAG = 4
+TAIL_GROUPS = 2
 WORDS = K // 2
 
 FLOPS = 2 * TOKENS * K * N
@@ -37,7 +38,7 @@ def tile_dcadecoderblock_pb_t_kernel(
     with (
         tc.tile_pool(name="const", bufs=1) as const,
         tc.tile_pool(name="resident", bufs=GROUPS) as resident,
-        tc.tile_pool(name="work", bufs=4) as work,
+        tc.tile_pool(name="work", bufs=5) as work,
         tc.tile_pool(name="stats", bufs=4) as stats,
         tc.psum_pool(name="psum_const", bufs=1) as psum_const,
         tc.psum_pool(name="psum_xt", bufs=3) as psum_xt,
@@ -45,7 +46,7 @@ def tile_dcadecoderblock_pb_t_kernel(
         tc.manual_schedule(),
     ):
         h_of, x_of, banks_of, grouped_of, codes_of, scales_of = {}, {}, {}, {}, {}, {}
-        acc_of, t_of, neg_mean_of, rstd_of, centred_of = {}, {}, {}, {}, {}
+        acc_of, t_of, neg_mean_of, rstd_of, centred_of, residual_of = {}, {}, {}, {}, {}, {}
 
         def load_h(g):
             h_of[g] = resident.tile([P, GROUP, K], BF16, name="h_sb")
@@ -82,6 +83,8 @@ def tile_dcadecoderblock_pb_t_kernel(
         nc.scalar.dma_start(out=rows[0:1, 2 * N : 3 * N], in_=attn_norm_g.unsqueeze(0))
         ident = const.tile([P, P], F32)
         make_identity(nc, ident[:])
+        ident_bf = const.tile([P, P], BF16)
+        make_identity(nc, ident_bf[:])
         ones = const.tile([P, P], BF16)
         nc.vector.memset(ones[:], 1.0)
         eps = const.tile([P, 1], F32)
@@ -191,24 +194,41 @@ def tile_dcadecoderblock_pb_t_kernel(
                 out=rstd_of[g][:], in_=sum_sq[:], func=ACT.Abs_reciprocal_sqrt, scale=1.0 / N, bias=eps[:]
             )
 
+        def residual_to_psum(g):
+            residual_of[g] = []
+            for pair in range(GROUP // PAIR):
+                bank = psum_acc.tile([P, PAIR, N], F32, name="acc")
+                residual_of[g].append(bank)
+                for jj in range(PAIR):
+                    nc.tensor.matmul(
+                        out=bank[:, jj, :], lhsT=ident_bf[:], rhs=x_of[g][:, pair * PAIR + jj, :],
+                        start=True, stop=False,
+                    )
+                    nc.tensor.matmul(
+                        out=bank[:, jj, :], lhsT=ones[:], rhs=rows[:, N : 2 * N], start=False, stop=True
+                    )
+
         def finish(g):
             o_sb = work.tile([P, GROUP, N], F32)
             for pair in range(GROUP // PAIR):
                 tiles = slice(pair * PAIR, (pair + 1) * PAIR)
-                for j in range(pair * PAIR, (pair + 1) * PAIR):
+                for jj in range(PAIR):
+                    j = pair * PAIR + jj
                     nc.vector.scalar_tensor_tensor(
                         out=o_sb[:, j, :], in0=centred_of[g][:, j, :], scalar=rstd_of[g][:, j : j + 1],
-                        in1=shift_bc, op0=ALU.mult, op1=ALU.add,
+                        in1=residual_of[g][pair][:, jj, :] if g in residual_of else shift_bc,
+                        op0=ALU.mult, op1=ALU.add,
                     )
-                nc.gpsimd.tensor_tensor(
-                    out=o_sb[:, tiles, :], in0=o_sb[:, tiles, :], in1=x_of[g][:, tiles, :], op=ALU.add
-                )
+                if g not in residual_of:
+                    nc.gpsimd.tensor_tensor(
+                        out=o_sb[:, tiles, :], in0=o_sb[:, tiles, :], in1=x_of[g][:, tiles, :], op=ALU.add
+                    )
                 nc.sync.dma_start(out=out_view[g][:, tiles, :], in_=o_sb[:, tiles, :])
 
         def live(g):
             return 0 <= g < GROUPS
 
-        for r in range(GROUPS + 5):
+        for r in range(GROUPS + 6):
             if live(r - 5):
                 deviation(r - 5)
             if live(r - 1):
@@ -218,10 +238,13 @@ def tile_dcadecoderblock_pb_t_kernel(
             if live(r - 4):
                 add_bias(r - 4)
                 mean(r - 4)
-            if live(r - 5):
-                centre_and_gain(r - 5)
+            if r - 4 == GROUPS - 1:
+                for g in range(GROUPS - TAIL_GROUPS, GROUPS):
+                    residual_to_psum(g)
+            if live(r - 6):
+                centre_and_gain(r - 6)
             if live(r - 2):
                 quantise(r - 2)
                 project(r - 2)
-            if live(r - 5):
-                finish(r - 5)
+            if live(r - 6):
+                finish(r - 6)

@@ -21,6 +21,11 @@ PAIR = 2
 GROUPS = TOKENS // (GROUP * P)
 X_LAG = 4
 TAIL_GROUPS = 2
+BODY_GROUPS = GROUPS - TAIL_GROUPS
+PAIRS = GROUP // PAIR
+SUMMED = 3
+EARLY_X_PER_H = 3
+VECTOR_SHARE = 5
 WORDS = K // 2
 
 FLOPS = 2 * TOKENS * K * N
@@ -38,8 +43,10 @@ def tile_dcadecoderblock_pb_t_kernel(
     with (
         tc.tile_pool(name="const", bufs=1) as const,
         tc.tile_pool(name="resident", bufs=GROUPS) as resident,
+        tc.tile_pool(name="resident_x", bufs=GROUPS * PAIRS) as resident_x,
+        tc.tile_pool(name="resident_xs", bufs=BODY_GROUPS) as resident_xs,
         tc.tile_pool(name="work", bufs=5) as work,
-        tc.tile_pool(name="stats", bufs=4) as stats,
+        tc.tile_pool(name="stats", bufs=6) as stats,
         tc.psum_pool(name="psum_const", bufs=1) as psum_const,
         tc.psum_pool(name="psum_xt", bufs=3) as psum_xt,
         tc.psum_pool(name="psum_acc", bufs=4) as psum_acc,
@@ -47,14 +54,15 @@ def tile_dcadecoderblock_pb_t_kernel(
     ):
         h_of, x_of, banks_of, grouped_of, codes_of, scales_of = {}, {}, {}, {}, {}, {}
         acc_of, t_of, neg_mean_of, rstd_of, centred_of, residual_of = {}, {}, {}, {}, {}, {}
+        sums_of, x_shifted_of, o_of = {}, {}, {}
 
         def load_h(g):
             h_of[g] = resident.tile([P, GROUP, K], BF16, name="h_sb")
             nc.sync.dma_start(out=h_of[g][:], in_=h_view[g])
 
-        def load_x(g):
-            x_of[g] = resident.tile([P, GROUP, N], BF16, name="x_sb")
-            nc.sync.dma_start(out=x_of[g][:], in_=x_view[g])
+        def load_x(g, pair):
+            x_of[g, pair] = resident_x.tile([P, PAIR, N], BF16, name="x_sb")
+            nc.sync.dma_start(out=x_of[g, pair][:], in_=x_view[g][:, pair * PAIR : (pair + 1) * PAIR, :])
 
         load_h(0)
         w_words = const.tile([P, 2 * N], U8, align_bytes=64)
@@ -70,11 +78,21 @@ def tile_dcadecoderblock_pb_t_kernel(
                 out=w_scales[32 * quadrant : 32 * quadrant + 4, :].bitcast(I32),
                 in_=scale_rows[4 * quadrant : 4 * quadrant + 4, :].bitcast(I32),
             )
+        pool_share = list(range(BODY_GROUPS - VECTOR_SHARE))
+        vector_share = list(range(BODY_GROUPS - VECTOR_SHARE, BODY_GROUPS))
+        early = []
+        for i in range(BODY_GROUPS):
+            early.extend(pool_share[i : i + 1])
+            early.extend(vector_share[i : i + 1])
         for g in range(1, GROUPS + X_LAG):
             if g < GROUPS:
                 load_h(g)
+            for e in early[(g - 1) * EARLY_X_PER_H : g * EARLY_X_PER_H]:
+                load_x(e, 1)
             if g >= X_LAG:
-                load_x(g - X_LAG)
+                load_x(g - X_LAG, 0)
+                if g - X_LAG >= BODY_GROUPS:
+                    load_x(g - X_LAG, 1)
 
         rows = const.tile([P, 3 * N], BF16)
         nc.vector.memset(rows[:], 0.0)
@@ -103,6 +121,17 @@ def tile_dcadecoderblock_pb_t_kernel(
         )
         shift_bc = shift_gain[:, 0, :]
         gain_bc = shift_gain[:, 1, :]
+        shift_sb = const.tile([P, 1, N], F32)
+        nc.vector.tensor_copy(out=shift_sb[:, 0, :], in_=shift_bc)
+
+        def shift_x(g, engine, shift):
+            x_shifted_of[g] = resident_xs.tile([P, PAIR, N], F32, name="x_shifted")
+            engine.tensor_tensor(
+                out=x_shifted_of[g][:], in0=x_of[g, 1][:], in1=shift.to_broadcast([P, PAIR, N]), op=ALU.add
+            )
+
+        for g in pool_share:
+            shift_x(g, nc.gpsimd, shift_sb[:])
 
         def transpose(g):
             h_words = h_of[g][:].bitcast(F32)
@@ -155,26 +184,42 @@ def tile_dcadecoderblock_pb_t_kernel(
 
         def add_bias(g):
             t_of[g] = work.tile([P, GROUP, N], F32, name="t")
-            for pair in range(GROUP // PAIR):
-                nc.vector.tensor_tensor(
-                    out=t_of[g][:, pair * PAIR : (pair + 1) * PAIR, :],
-                    in0=acc_of[g][pair][:],
-                    in1=bias_bc[:].to_broadcast([P, PAIR, N]),
-                    op=ALU.add,
-                )
+            sums_of[g] = stats.tile([P, GROUP], F32, name="sums")
+            for pair in range(PAIRS):
+                if (pair + 1) * PAIR <= GROUP - SUMMED:
+                    nc.vector.tensor_tensor(
+                        out=t_of[g][:, pair * PAIR : (pair + 1) * PAIR, :],
+                        in0=acc_of[g][pair][:],
+                        in1=bias_bc[:].to_broadcast([P, PAIR, N]),
+                        op=ALU.add,
+                    )
+                    continue
+                for jj in range(PAIR):
+                    j = pair * PAIR + jj
+                    nc.vector.scalar_tensor_tensor(
+                        out=t_of[g][:, j, :], in0=acc_of[g][pair][:, jj, :], scalar=1.0,
+                        in1=bias_bc[:, 0, :], op0=ALU.mult, op1=ALU.add,
+                        accum_out=sums_of[g][:, j : j + 1] if j >= GROUP - SUMMED else None,
+                    )
 
         def mean(g):
             neg_mean_of[g] = stats.tile([P, GROUP], F32, name="neg_mean")
-            for j in range(GROUP):
+            for j in range(GROUP - SUMMED):
                 unread = stats.tile([P, N], BF16, name="unread")
                 nc.scalar.activation(
                     out=unread[:], in_=t_of[g][:, j, :], func=ACT.Identity, scale=-1.0 / N,
                     accum_out=neg_mean_of[g][:, j : j + 1],
                 )
 
+        def mean_of_sums(g):
+            summed = slice(GROUP - SUMMED, GROUP)
+            nc.scalar.activation(
+                out=neg_mean_of[g][:, summed], in_=sums_of[g][:, summed], func=ACT.Identity, scale=-1.0 / N
+            )
+
         def centre_and_gain(g):
             centred_of[g] = work.tile([P, GROUP, N], F32, name="centred")
-            for j in range(GROUP):
+            for j in (2, 3, 0, 1):
                 nc.vector.scalar_tensor_tensor(
                     out=centred_of[g][:, j, :], in0=t_of[g][:, j, :],
                     scalar=neg_mean_of[g][:, j : j + 1], in1=gain_bc,
@@ -201,35 +246,46 @@ def tile_dcadecoderblock_pb_t_kernel(
                 residual_of[g].append(bank)
                 for jj in range(PAIR):
                     nc.tensor.matmul(
-                        out=bank[:, jj, :], lhsT=ident_bf[:], rhs=x_of[g][:, pair * PAIR + jj, :],
+                        out=bank[:, jj, :], lhsT=ident_bf[:], rhs=x_of[g, pair][:, jj, :],
                         start=True, stop=False,
                     )
                     nc.tensor.matmul(
                         out=bank[:, jj, :], lhsT=ones[:], rhs=rows[:, N : 2 * N], start=False, stop=True
                     )
 
-        def finish(g):
-            o_sb = work.tile([P, GROUP, N], F32)
-            for pair in range(GROUP // PAIR):
-                tiles = slice(pair * PAIR, (pair + 1) * PAIR)
-                for jj in range(PAIR):
-                    j = pair * PAIR + jj
-                    nc.vector.scalar_tensor_tensor(
-                        out=o_sb[:, j, :], in0=centred_of[g][:, j, :], scalar=rstd_of[g][:, j : j + 1],
-                        in1=residual_of[g][pair][:, jj, :] if g in residual_of else shift_bc,
-                        op0=ALU.mult, op1=ALU.add,
-                    )
-                if g not in residual_of:
-                    nc.gpsimd.tensor_tensor(
-                        out=o_sb[:, tiles, :], in0=o_sb[:, tiles, :], in1=x_of[g][:, tiles, :], op=ALU.add
-                    )
-                nc.sync.dma_start(out=out_view[g][:, tiles, :], in_=o_sb[:, tiles, :])
+        def finish_off_vector(g):
+            tiles = slice(PAIR, GROUP)
+            for j in range(PAIR, GROUP):
+                nc.scalar.activation(
+                    out=o_of[g][:, j, :], in_=centred_of[g][:, j, :], func=ACT.Identity,
+                    scale=rstd_of[g][:, j : j + 1],
+                )
+            nc.gpsimd.tensor_tensor(
+                out=o_of[g][:, tiles, :], in0=o_of[g][:, tiles, :], in1=x_shifted_of[g][:], op=ALU.add
+            )
+            nc.sync.dma_start(out=out_view[g][:, tiles, :], in_=o_of[g][:, tiles, :])
+
+        def finish(g, pair):
+            tiles = slice(pair * PAIR, (pair + 1) * PAIR)
+            for jj in range(PAIR):
+                j = pair * PAIR + jj
+                nc.vector.scalar_tensor_tensor(
+                    out=o_of[g][:, j, :], in0=centred_of[g][:, j, :], scalar=rstd_of[g][:, j : j + 1],
+                    in1=residual_of[g][pair][:, jj, :] if g in residual_of else shift_bc,
+                    op0=ALU.mult, op1=ALU.add,
+                )
+            if g not in residual_of:
+                nc.gpsimd.tensor_tensor(
+                    out=o_of[g][:, tiles, :], in0=o_of[g][:, tiles, :], in1=x_of[g, pair][:], op=ALU.add
+                )
+            nc.sync.dma_start(out=out_view[g][:, tiles, :], in_=o_of[g][:, tiles, :])
 
         def live(g):
             return 0 <= g < GROUPS
 
         for r in range(GROUPS + 6):
             if live(r - 5):
+                mean_of_sums(r - 5)
                 deviation(r - 5)
             if live(r - 1):
                 regroup(r - 1)
@@ -243,8 +299,15 @@ def tile_dcadecoderblock_pb_t_kernel(
                     residual_to_psum(g)
             if live(r - 6):
                 centre_and_gain(r - 6)
+                o_of[r - 6] = work.tile([P, GROUP, N], F32, name="o_sb")
+                if r - 6 < BODY_GROUPS:
+                    finish_off_vector(r - 6)
             if live(r - 2):
                 quantise(r - 2)
                 project(r - 2)
+            for g in vector_share[(r - 2) * 2 : (r - 1) * 2] if r >= 2 else []:
+                shift_x(g, nc.vector, shift_gain[:, 0:1, :])
             if live(r - 6):
-                finish(r - 6)
+                finish(r - 6, 0)
+                if r - 6 >= BODY_GROUPS:
+                    finish(r - 6, 1)

@@ -219,7 +219,7 @@ def tile_dcadecoderblock_pb_t_kernel(
 
         def centre_and_gain(g):
             centred_of[g] = work.tile([P, GROUP, N], F32, name="centred")
-            for j in (2, 3, 0, 1):
+            for j in range(GROUP):
                 nc.vector.scalar_tensor_tensor(
                     out=centred_of[g][:, j, :], in0=t_of[g][:, j, :],
                     scalar=neg_mean_of[g][:, j : j + 1], in1=gain_bc,

import concourse.mybir as mybir
from concourse.masks import make_identity

F32 = mybir.dt.float32
BF16 = mybir.dt.bfloat16
I32 = mybir.dt.int32
U32 = mybir.dt.uint32
U8 = mybir.dt.uint8
FP8X4 = mybir.dt.float8_e4m3fn_x4
FP4X4 = mybir.dt.float4_e2m1fn_x4
ALU = mybir.AluOpType
ACT = mybir.ActivationFunctionType

P = 128
TOKENS = 4 * 2048
K = 512
N = 256
EPS = 1e-5
GROUP = 4
PAIR = 2
GROUPS = TOKENS // (GROUP * P)
X_LAG = 4
TAIL_GROUPS = 2
BODY_GROUPS = GROUPS - TAIL_GROUPS
PAIRS = GROUP // PAIR
SUMMED = 3
EARLY_X_PER_H = 3
VECTOR_SHARE = 5
WORDS = K // 2

FLOPS = 2 * TOKENS * K * N


def tile_dcadecoderblock_pb_t_kernel(
    tc, h_attn, x, attn_out_W_words, attn_out_W_scales, attn_out_b, attn_norm_g, attn_norm_b, out
):
    nc = tc.nc

    h_view = h_attn.flatten_outer_dims().rearrange("(g p j) k -> g p j k", p=P, j=GROUP)
    x_view = x.flatten_outer_dims().rearrange("(g p j) n -> g p j n", p=P, j=GROUP)
    out_view = out.flatten_outer_dims().rearrange("(g p j) n -> g p j n", p=P, j=GROUP)

    with (
        tc.tile_pool(name="const", bufs=1) as const,
        tc.tile_pool(name="resident", bufs=GROUPS) as resident,
        tc.tile_pool(name="resident_x", bufs=GROUPS * PAIRS) as resident_x,
        tc.tile_pool(name="resident_xs", bufs=BODY_GROUPS) as resident_xs,
        tc.tile_pool(name="work", bufs=5) as work,
        tc.tile_pool(name="stats", bufs=6) as stats,
        tc.psum_pool(name="psum_const", bufs=1) as psum_const,
        tc.psum_pool(name="psum_xt", bufs=3) as psum_xt,
        tc.psum_pool(name="psum_acc", bufs=4) as psum_acc,
        tc.manual_schedule(),
    ):
        h_of, x_of, banks_of, grouped_of, codes_of, scales_of = {}, {}, {}, {}, {}, {}
        acc_of, t_of, neg_mean_of, rstd_of, centred_of, residual_of = {}, {}, {}, {}, {}, {}
        sums_of, x_shifted_of, o_of = {}, {}, {}

        def load_h(g):
            h_of[g] = resident.tile([P, GROUP, K], BF16, name="h_sb")
            nc.sync.dma_start(out=h_of[g][:], in_=h_view[g])

        def load_x(g, pair):
            x_of[g, pair] = resident_x.tile([P, PAIR, N], BF16, name="x_sb")
            nc.sync.dma_start(out=x_of[g, pair][:], in_=x_view[g][:, pair * PAIR : (pair + 1) * PAIR, :])

        load_h(0)
        w_words = const.tile([P, 2 * N], U8, align_bytes=64)
        nc.sync.dma_start(
            out=w_words[:].bitcast(I32),
            in_=attn_out_W_words.rearrange("g p b -> (g p) b").bitcast(I32),
        )
        w_scales = const.tile([P, N], U8, align_bytes=64)
        nc.vector.memset(w_scales[:].bitcast(I32), 0)
        scale_rows = attn_out_W_scales.rearrange("g q n -> (g q) n")
        for quadrant in range(4):
            nc.sync.dma_start(
                out=w_scales[32 * quadrant : 32 * quadrant + 4, :].bitcast(I32),
                in_=scale_rows[4 * quadrant : 4 * quadrant + 4, :].bitcast(I32),
            )
        pool_share = list(range(BODY_GROUPS - VECTOR_SHARE))
        vector_share = list(range(BODY_GROUPS - VECTOR_SHARE, BODY_GROUPS))
        early = []
        for i in range(BODY_GROUPS):
            early.extend(pool_share[i : i + 1])
            early.extend(vector_share[i : i + 1])
        for g in range(1, GROUPS + X_LAG):
            if g < GROUPS:
                load_h(g)
            for e in early[(g - 1) * EARLY_X_PER_H : g * EARLY_X_PER_H]:
                load_x(e, 1)
            if g >= X_LAG:
                load_x(g - X_LAG, 0)
                if g - X_LAG >= BODY_GROUPS:
                    load_x(g - X_LAG, 1)

        rows = const.tile([P, 3 * N], BF16)
        nc.vector.memset(rows[:], 0.0)
        nc.scalar.dma_start(out=rows[0:1, 0:N], in_=attn_out_b.unsqueeze(0))
        nc.scalar.dma_start(out=rows[0:1, N : 2 * N], in_=attn_norm_b.unsqueeze(0))
        nc.scalar.dma_start(out=rows[0:1, 2 * N : 3 * N], in_=attn_norm_g.unsqueeze(0))
        ident = const.tile([P, P], F32)
        make_identity(nc, ident[:])
        ident_bf = const.tile([P, P], BF16)
        make_identity(nc, ident_bf[:])
        ones = const.tile([P, P], BF16)
        nc.vector.memset(ones[:], 1.0)
        eps = const.tile([P, 1], F32)
        nc.vector.memset(eps[:], EPS)
        warm = const.tile([P, 1], F32)
        nc.scalar.activation(out=warm[:], in_=eps[:], func=ACT.Abs_reciprocal_sqrt)

        spread = psum_acc.tile([P, PAIR, N], F32, name="acc")
        nc.tensor.matmul(out=spread[:, 0, :], lhsT=ones[:], rhs=rows[:, 0:N], start=True, stop=True)
        bias_bc = const.tile([P, 1, N], F32)
        nc.vector.tensor_copy(out=bias_bc[:, 0, :], in_=spread[:, 0, :])
        shift_gain = psum_const.tile([P, 2, N], F32)
        nc.tensor.matmul(
            out=shift_gain[:].rearrange("p a n -> p (a n)"), lhsT=ones[:], rhs=rows[:, N : 3 * N],
            start=True, stop=True,
        )
        shift_bc = shift_gain[:, 0, :]
        gain_bc = shift_gain[:, 1, :]
        shift_sb = const.tile([P, 1, N], F32)
        nc.vector.tensor_copy(out=shift_sb[:, 0, :], in_=shift_bc)

        def shift_x(g, engine, shift):
            x_shifted_of[g] = resident_xs.tile([P, PAIR, N], F32, name="x_shifted")
            engine.tensor_tensor(
                out=x_shifted_of[g][:], in0=x_of[g, 1][:], in1=shift.to_broadcast([P, PAIR, N]), op=ALU.add
            )

        for g in pool_share:
            shift_x(g, nc.gpsimd, shift_sb[:])

        def transpose(g):
            h_words = h_of[g][:].bitcast(F32)
            banks_of[g] = []
            for pair in range(GROUP // PAIR):
                xt = psum_xt.tile([P, 2, PAIR * P], F32)
                banks_of[g].append(xt)
                for jj in range(PAIR):
                    for u in range(2):
                        nc.tensor.transpose(
                            xt[:, u, jj * P : (jj + 1) * P],
                            h_words[:, pair * PAIR + jj, u:WORDS:2],
                            ident[:],
                        )

        def regroup(g):
            grouped_of[g] = work.tile([P, GROUP * P * 4], BF16, align_bytes=64, name="grouped")
            grouped_words = grouped_of[g][:].bitcast(F32)
            for pair in range(GROUP // PAIR):
                nc.scalar.copy(
                    out=grouped_words[:, pair * 4 * P : (pair + 1) * 4 * P].rearrange(
                        "p (c u) -> p c u", u=2
                    ),
                    in_=banks_of[g][pair][:].rearrange("p u c -> p c u"),
                )

        def quantise(g):
            codes_of[g] = work.tile([P, GROUP * P], U32, align_bytes=64, name="codes")
            scales_of[g] = work.tile([P, GROUP * P], U8, align_bytes=64, name="scales")
            nc.vector.quantize_mx(
                out=codes_of[g][:].bitcast(FP8X4), scales=scales_of[g][:], in_=grouped_of[g][:]
            )

        def project(g):
            acc_of[g] = []
            for pair in range(GROUP // PAIR):
                acc = psum_acc.tile([P, PAIR, N], F32)
                acc_of[g].append(acc)
                for jj in range(PAIR):
                    cols = slice((pair * PAIR + jj) * P, (pair * PAIR + jj + 1) * P)
                    nc.tensor.matmul_mx(
                        out=acc[:, jj, :],
                        lhsT=codes_of[g][:, cols].bitcast(FP8X4),
                        lhsT_scale=scales_of[g][:, cols],
                        rhs=w_words[:].bitcast(FP4X4),
                        rhs_scale=w_scales[:],
                        start=True,
                        stop=True,
                    )

        def add_bias(g):
            t_of[g] = work.tile([P, GROUP, N], F32, name="t")
            sums_of[g] = stats.tile([P, GROUP], F32, name="sums")
            for pair in range(PAIRS):
                if (pair + 1) * PAIR <= GROUP - SUMMED:
                    nc.vector.tensor_tensor(
                        out=t_of[g][:, pair * PAIR : (pair + 1) * PAIR, :],
                        in0=acc_of[g][pair][:],
                        in1=bias_bc[:].to_broadcast([P, PAIR, N]),
                        op=ALU.add,
                    )
                    continue
                for jj in range(PAIR):
                    j = pair * PAIR + jj
                    nc.vector.scalar_tensor_tensor(
                        out=t_of[g][:, j, :], in0=acc_of[g][pair][:, jj, :], scalar=1.0,
                        in1=bias_bc[:, 0, :], op0=ALU.mult, op1=ALU.add,
                        accum_out=sums_of[g][:, j : j + 1] if j >= GROUP - SUMMED else None,
                    )

        def mean(g):
            neg_mean_of[g] = stats.tile([P, GROUP], F32, name="neg_mean")
            for j in range(GROUP - SUMMED):
                unread = stats.tile([P, N], BF16, name="unread")
                nc.scalar.activation(
                    out=unread[:], in_=t_of[g][:, j, :], func=ACT.Identity, scale=-1.0 / N,
                    accum_out=neg_mean_of[g][:, j : j + 1],
                )

        def mean_of_sums(g):
            summed = slice(GROUP - SUMMED, GROUP)
            nc.scalar.activation(
                out=neg_mean_of[g][:, summed], in_=sums_of[g][:, summed], func=ACT.Identity, scale=-1.0 / N
            )

        def centre_and_gain(g):
            centred_of[g] = work.tile([P, GROUP, N], F32, name="centred")
            for j in range(GROUP):
                nc.vector.scalar_tensor_tensor(
                    out=centred_of[g][:, j, :], in0=t_of[g][:, j, :],
                    scalar=neg_mean_of[g][:, j : j + 1], in1=gain_bc,
                    op0=ALU.add, op1=ALU.mult,
                )

        def deviation(g):
            sum_sq = stats.tile([P, GROUP], F32)
            for j in range(GROUP):
                unread = stats.tile([P, N], BF16, name="unread")
                nc.scalar.activation(
                    out=unread[:], in_=t_of[g][:, j, :], func=ACT.Square,
                    bias=neg_mean_of[g][:, j : j + 1], accum_out=sum_sq[:, j : j + 1],
                )
            rstd_of[g] = stats.tile([P, GROUP], F32, name="rstd")
            nc.scalar.activation(
                out=rstd_of[g][:], in_=sum_sq[:], func=ACT.Abs_reciprocal_sqrt, scale=1.0 / N, bias=eps[:]
            )

        def residual_to_psum(g):
            residual_of[g] = []
            for pair in range(GROUP // PAIR):
                bank = psum_acc.tile([P, PAIR, N], F32, name="acc")
                residual_of[g].append(bank)
                for jj in range(PAIR):
                    nc.tensor.matmul(
                        out=bank[:, jj, :], lhsT=ident_bf[:], rhs=x_of[g, pair][:, jj, :],
                        start=True, stop=False,
                    )
                    nc.tensor.matmul(
                        out=bank[:, jj, :], lhsT=ones[:], rhs=rows[:, N : 2 * N], start=False, stop=True
                    )

        def finish_off_vector(g):
            tiles = slice(PAIR, GROUP)
            for j in range(PAIR, GROUP):
                nc.scalar.activation(
                    out=o_of[g][:, j, :], in_=centred_of[g][:, j, :], func=ACT.Identity,
                    scale=rstd_of[g][:, j : j + 1],
                )
            nc.gpsimd.tensor_tensor(
                out=o_of[g][:, tiles, :], in0=o_of[g][:, tiles, :], in1=x_shifted_of[g][:], op=ALU.add
            )
            nc.sync.dma_start(out=out_view[g][:, tiles, :], in_=o_of[g][:, tiles, :])

        def finish(g, pair):
            tiles = slice(pair * PAIR, (pair + 1) * PAIR)
            for jj in range(PAIR):
                j = pair * PAIR + jj
                nc.vector.scalar_tensor_tensor(
                    out=o_of[g][:, j, :], in0=centred_of[g][:, j, :], scalar=rstd_of[g][:, j : j + 1],
                    in1=residual_of[g][pair][:, jj, :] if g in residual_of else shift_bc,
                    op0=ALU.mult, op1=ALU.add,
                )
            if g not in residual_of:
                nc.gpsimd.tensor_tensor(
                    out=o_of[g][:, tiles, :], in0=o_of[g][:, tiles, :], in1=x_of[g, pair][:], op=ALU.add
                )
            nc.sync.dma_start(out=out_view[g][:, tiles, :], in_=o_of[g][:, tiles, :])

        def live(g):
            return 0 <= g < GROUPS

        for r in range(GROUPS + 6):
            if live(r - 5):
                mean_of_sums(r - 5)
                deviation(r - 5)
            if live(r - 1):
                regroup(r - 1)
            if live(r):
                transpose(r)
            if live(r - 4):
                add_bias(r - 4)
                mean(r - 4)
            if r - 4 == GROUPS - 1:
                for g in range(GROUPS - TAIL_GROUPS, GROUPS):
                    residual_to_psum(g)
            if live(r - 6):
                centre_and_gain(r - 6)
                o_of[r - 6] = work.tile([P, GROUP, N], F32, name="o_sb")
                if r - 6 < BODY_GROUPS:
                    finish_off_vector(r - 6)
            if live(r - 2):
                quantise(r - 2)
                project(r - 2)
            for g in vector_share[(r - 2) * 2 : (r - 1) * 2] if r >= 2 else []:
                shift_x(g, nc.vector, shift_gain[:, 0:1, :])
            if live(r - 6):
                finish(r - 6, 0)
                if r - 6 >= BODY_GROUPS:
                    finish(r - 6, 1)
